import numpy as np
import ml_dtypes


def mxq(x, axis, fmt="e4m3"):
    dtype, down = {"e4m3": (ml_dtypes.float8_e4m3fn, 7), "e5m2": (ml_dtypes.float8_e5m2, 14)}[fmt]
    v = np.moveaxis(np.asarray(x, np.float32).astype(ml_dtypes.bfloat16).astype(np.float64), axis, -1)
    blocks = v.reshape(v.shape[:-1] + (-1, 32))
    amax = np.abs(blocks).max(-1, keepdims=True)
    byte = np.maximum(np.where(amax > 0, np.frexp(amax)[1] - 1 + 127, 0) - down, 1)
    scale = np.exp2(byte - 127.0)
    codes = (blocks / scale).astype(np.float32).astype(dtype).astype(np.float64)
    return np.moveaxis((codes * scale).reshape(v.shape), -1, axis)


WIDE = False


def mx_kscale(k):
    if not WIDE:
        return np.ones(k)
    levels = np.array([10, -10, 5, -5, 0])
    a = np.random.permutation(np.resize(levels, k // 512 * 4)).reshape(k // 512, 4)
    idx = np.arange(k)
    return np.exp2(a[idx // 512, idx % 128 // 32])


BF16 = ml_dtypes.bfloat16


def bf(x):
    return np.asarray(x, np.float32).astype(BF16)


def f64(x):
    return np.asarray(x).astype(np.float64)


B, NI, NK, NJ, C_Z, C_H = 1, 512, 512, 512, 128, 8
EPS = 1e-5
KEEP = 0.85


def layer_norm(x, w, b):
    mu = x.mean(-1, keepdims=True)
    var = ((x - mu) ** 2).mean(-1, keepdims=True)
    return (x - mu) / np.sqrt(var + EPS) * w + b


def setup_inputs():
    s = mx_kscale(NK)
    return {"a_gated": bf(np.random.standard_normal((B, NI, NK, C_H)) * 0.55 * s[None, None, :, None]),
            "b_gated": bf(np.random.standard_normal((B, NK, NJ, C_H)) * 0.55 / s[None, :, None, None]),
            "mask_ik": bf(np.random.random((B, NI, NK)) < KEEP),
            "mask_kj": bf(np.random.random((B, NK, NJ)) < KEEP),
            "ln_out_w": bf(1.0 + 0.1 * np.random.standard_normal(C_H)),
            "ln_out_b": bf(0.1 * np.random.standard_normal(C_H))}


def reference(a_gated, b_gated, mask_ik, mask_kj, ln_out_w, ln_out_b):
    a = f64(mask_ik)[..., None] * f64(a_gated)
    b = f64(mask_kj)[..., None] * f64(b_gated)
    at = a.transpose(0, 3, 1, 2)
    bt = b.transpose(0, 3, 1, 2)
    x = (mxq(at, 3, "e4m3") @ mxq(bt, 2, "e4m3")).transpose(0, 2, 3, 1)
    return layer_norm(x, f64(ln_out_w), f64(ln_out_b))

@@ -1,0 +1,240 @@
+from contextlib import ExitStack
+
+import concourse.mybir as mybir
+from concourse.masks import make_identity
+
+FP8X4 = mybir.dt.float8_e4m3fn_x4
+BF16 = mybir.dt.bfloat16
+F32 = mybir.dt.float32
+U32 = mybir.dt.uint32
+U8 = mybir.dt.uint8
+ALU = mybir.AluOpType
+ACT = mybir.ActivationFunctionType
+
+P = 128
+PACK = 4
+NI = 512
+NK = P * PACK
+NJ = 512
+ND = 8
+I_TILES = NI // P
+JC = 128
+J_CHUNKS = NJ // JC
+HALF = ND // 2
+EPS = 1e-5
+
+FLOPS = 2 * NI * NJ * NK * ND
+
+
+def tile_trianglemultiplicativeupdate_pa_kernel(
+    tc, a_gated, b_gated, mask_ik, mask_kj, ln_out_w, ln_out_b, out
+):
+    nc = tc.nc
+
+    a_rows = a_gated.rearrange("b (n p) k d -> (b n) p (k d)", p=P)
+    mik_rows = mask_ik.rearrange("b (n p) k -> p (b n) k", p=P)
+    b_rows = b_gated.rearrange("b (t p) j d -> p (b t) (j d)", p=P)
+    mkj_rows = mask_kj.rearrange("b (t p) j -> p (b t) j", p=P)
+    out_rows = out.rearrange("b (n p) j d -> (b n) p (j d)", p=P)
+
+    with ExitStack() as ctx:
+        consts = ctx.enter_context(tc.tile_pool(name="consts", bufs=1))
+        keep = ctx.enter_context(tc.tile_pool(name="keep", bufs=1))
+        a_in = ctx.enter_context(tc.tile_pool(name="a_in", bufs=3))
+        a_work = ctx.enter_context(tc.tile_pool(name="a_work", bufs=2))
+        b_in = ctx.enter_context(tc.tile_pool(name="b_in", bufs=3))
+        b_work = ctx.enter_context(tc.tile_pool(name="b_work", bufs=2))
+        b_mx = ctx.enter_context(tc.tile_pool(name="b_mx", bufs=3))
+        ln = ctx.enter_context(tc.tile_pool(name="ln", bufs=3))
+        results = ctx.enter_context(tc.tile_pool(name="results", bufs=4))
+        psum = ctx.enter_context(tc.psum_pool(name="psum", bufs=8))
+
+        ident_f32 = consts.tile([P, P], F32)
+        make_identity(nc, ident_f32[:])
+        ident_bf16 = consts.tile([P, P], BF16)
+        make_identity(nc, ident_bf16[:])
+        w_bf16 = consts.tile([P, ND], BF16)
+        nc.scalar.dma_start(out=w_bf16[:], in_=ln_out_w.partition_broadcast(P))
+        bias_bf16 = consts.tile([P, ND], BF16)
+        nc.scalar.dma_start(out=bias_bf16[:], in_=ln_out_b.partition_broadcast(P))
+        w_col = consts.tile([P, ND], F32)
+        nc.vector.tensor_copy(out=w_col[:], in_=w_bf16[:])
+        bias_col = consts.tile([P, ND], F32)
+        nc.vector.tensor_copy(out=bias_col[:], in_=bias_bf16[:])
+        eps_col = consts.tile([P, 1], F32)
+        nc.vector.memset(eps_col[:], EPS)
+
+        mik = keep.tile([P, I_TILES, NK], BF16)
+        nc.sync.dma_start(out=mik[:], in_=mik_rows)
+        mkj = keep.tile([P, PACK, NJ], BF16)
+
+        a_raw_tiles = []
+        b_raw_tiles = []
+
+        def load_a(it):
+            a_raw = a_in.tile([P, NK * ND], BF16)
+            nc.sync.dma_start(out=a_raw[:], in_=a_rows[it])
+            a_raw_tiles.append(a_raw)
+
+        def load_b(jc):
+            b_raw = b_in.tile([P, PACK, JC * ND], BF16)
+            nc.sync.dma_start(out=b_raw[:], in_=b_rows[:, :, jc * JC * ND : (jc + 1) * JC * ND])
+            b_raw_tiles.append(b_raw)
+
+        load_a(0)
+        load_a(1)
+        nc.sync.dma_start(out=mkj[:], in_=mkj_rows)
+        load_b(0)
+        load_a(2)
+
+        a_codes = keep.tile([P, I_TILES, ND * P], U32, align_bytes=64)
+        a_scales = keep.tile([P, I_TILES, ND * P], U8, align_bytes=64)
+        mikT = keep.tile([P, I_TILES, P, PACK], BF16)
+
+        def prepare_a(it):
+            a_raw = a_raw_tiles[it]
+            maskT_ps = psum.tile([P, PACK, P], BF16, tag="bank")
+            for t in range(PACK):
+                nc.tensor.transpose(maskT_ps[:, t, :], mik[:, it, t * P : (t + 1) * P], ident_bf16[:])
+            nc.vector.tensor_copy(out=mikT[:, it, :, :], in_=maskT_ps[:].rearrange("p t i -> p i t"))
+
+            a_words = a_raw[:].bitcast(F32).rearrange("p (k w) -> p k w", w=ND // 2)
+            a_grouped = a_work.tile([P, ND, P, PACK], BF16, align_bytes=64)
+            for w in range(ND // 2):
+                aT_ps = psum.tile([P, PACK * P], F32, tag="bank")
+                for t in range(PACK):
+                    nc.tensor.transpose(aT_ps[:, t * P : (t + 1) * P], a_words[:, t * P : (t + 1) * P, w], ident_f32[:])
+                nc.scalar.copy(
+                    out=a_grouped[:, 2 * w : 2 * w + 2, :, :],
+                    in_=aT_ps[:].bitcast(BF16).rearrange("p (t i e) -> p e i t", t=PACK, e=2),
+                )
+            a_flat = a_grouped[:].rearrange("p d i t -> p d (i t)")
+            nc.vector.tensor_tensor(
+                out=a_flat,
+                in0=a_flat,
+                in1=mikT[:, it, :, :].rearrange("p i t -> p (i t)").unsqueeze(1).to_broadcast([P, ND, P * PACK]),
+                op=ALU.mult,
+            )
+            nc.vector.quantize_mx(
+                out=a_codes[:, it, :].bitcast(FP8X4),
+                scales=a_scales[:, it, :],
+                in_=a_grouped[:].rearrange("p d i t -> p (d i t)"),
+            )
+
+        mkj_grouped = keep.tile([P, NJ, PACK], BF16)
+
+        def prepare_b(jc):
+            b_raw = b_raw_tiles[jc]
+            b_grouped = b_work.tile([P, ND, JC, PACK], BF16, align_bytes=64)
+            src = b_raw[:].rearrange("p t (j d) -> p j t d", d=ND)
+            dst = b_grouped[:].rearrange("p d j t -> p j t d")
+            for h in range(2):
+                half = slice(h * HALF, (h + 1) * HALF)
+                nc.scalar.copy(out=dst[:, :, :, half], in_=src[:, :, :, half])
+            b_flat = b_grouped[:].rearrange("p d j t -> p d (j t)")
+            nc.vector.tensor_tensor(
+                out=b_flat,
+                in0=b_flat,
+                in1=mkj_grouped[:, jc * JC : (jc + 1) * JC, :]
+                .rearrange("p j t -> p (j t)")
+                .unsqueeze(1)
+                .to_broadcast([P, ND, JC * PACK]),
+                op=ALU.mult,
+            )
+            b_codes = b_mx.tile([P, ND, JC], U32, align_bytes=64)
+            b_scales = b_mx.tile([P, ND, JC], U8, align_bytes=64)
+            nc.vector.quantize_mx(
+                out=b_codes[:].rearrange("p d j -> p (d j)").bitcast(FP8X4),
+                scales=b_scales[:].rearrange("p d j -> p (d j)"),
+                in_=b_grouped[:].rearrange("p d j t -> p (d j t)"),
+            )
+            return b_codes, b_scales
+
+        def product_and_norm(it, jc, b_codes, b_scales):
+            sum_ps = psum.tile([P, JC], F32, tag="bank")
+            x_lo = psum.tile([P, HALF, JC], F32, tag="bank")
+            x_hi = psum.tile([P, HALF, JC], F32, tag="bank")
+            x_ps = [x_lo, x_hi]
+            for d in range(ND):
+                operands = dict(
+                    lhsT=a_codes[:, it, d * P : (d + 1) * P].bitcast(FP8X4),
+                    lhsT_scale=a_scales[:, it, d * P : (d + 1) * P],
+                    rhs=b_codes[:, d, :].bitcast(FP8X4),
+                    rhs_scale=b_scales[:, d, :],
+                )
+                nc.tensor.matmul_mx(out=x_ps[d // HALF][:, d % HALF, :], start=True, stop=True, **operands)
+                nc.tensor.matmul_mx(out=sum_ps[:], start=(d == 0), stop=(d == ND - 1), **operands)
+
+            mean = ln.tile([P, JC], F32)
+            nc.scalar.activation(out=mean[:], in_=sum_ps[:], func=ACT.Copy, scale=1.0 / ND)
+            mean_sq = ln.tile([P, JC], F32)
+            nc.scalar.activation(out=mean_sq[:], in_=sum_ps[:], func=ACT.Square, scale=1.0 / ND)
+            squares = ln.tile([P, ND, JC], F32)
+            for h in range(2):
+                nc.scalar.activation(
+                    out=squares[:, h * HALF : (h + 1) * HALF, :], in_=x_ps[h][:], func=ACT.Square
+                )
+            sum4 = ln.tile([P, 4, JC], F32)
+            nc.gpsimd.tensor_tensor(out=sum4[:], in0=squares[:, 0:4, :], in1=squares[:, 4:8, :], op=ALU.add)
+            sum2 = ln.tile([P, 2, JC], F32)
+            nc.gpsimd.tensor_tensor(out=sum2[:], in0=sum4[:, 0:2, :], in1=sum4[:, 2:4, :], op=ALU.add)
+            sum1 = ln.tile([P, JC], F32)
+            nc.gpsimd.tensor_tensor(out=sum1[:], in0=sum2[:, 0, :], in1=sum2[:, 1, :], op=ALU.add)
+
+            var = ln.tile([P, JC], F32)
+            nc.vector.scalar_tensor_tensor(
+                out=var[:], in0=sum1[:], scalar=1.0 / ND, in1=mean_sq[:], op0=ALU.mult, op1=ALU.subtract
+            )
+            rstd = ln.tile([P, JC], F32)
+            nc.scalar.activation(out=rstd[:], in_=var[:], func=ACT.Abs_reciprocal_sqrt, bias=eps_col[:, 0:1])
+            neg_mean_rstd = ln.tile([P, JC], F32)
+            nc.vector.scalar_tensor_tensor(
+                out=neg_mean_rstd[:], in0=mean[:], scalar=-1.0, in1=rstd[:], op0=ALU.mult, op1=ALU.mult
+            )
+
+            shift = ln.tile([P, ND, JC], F32)
+            scaled = ln.tile([P, ND, JC], F32)
+            for d in range(ND):
+                nc.scalar.activation(
+                    out=shift[:, d, :],
+                    in_=neg_mean_rstd[:],
+                    func=ACT.Identity,
+                    scale=w_col[:, d : d + 1],
+                    bias=bias_col[:, d : d + 1],
+                )
+                nc.vector.scalar_tensor_tensor(
+                    out=scaled[:, d, :],
+                    in0=x_ps[d // HALF][:, d % HALF, :],
+                    scalar=w_col[:, d : d + 1],
+                    in1=rstd[:],
+                    op0=ALU.mult,
+                    op1=ALU.mult,
+                )
+            result = results.tile([P, JC, ND], F32)
+            for h in range(2):
+                half = slice(h * HALF, (h + 1) * HALF)
+                nc.vector.tensor_tensor(
+                    out=result[:, :, half],
+                    in0=scaled[:, half, :].rearrange("p d j -> p j d"),
+                    in1=shift[:, half, :].rearrange("p d j -> p j d"),
+                    op=ALU.add,
+                )
+            nc.sync.dma_start(
+                out=out_rows[it, :, jc * JC * ND : (jc + 1) * JC * ND],
+                in_=result[:].rearrange("p j d -> p (j d)"),
+            )
+
+        prepare_a(0)
+        load_a(3)
+        prepare_a(1)
+        load_b(1)
+        nc.vector.tensor_copy(out=mkj_grouped[:], in_=mkj[:].rearrange("p t j -> p j t"))
+        prepare_a(2)
+        load_b(2)
+        prepare_a(3)
+        for jc in range(J_CHUNKS):
+            b_codes, b_scales = prepare_b(jc)
+            if jc + 3 < J_CHUNKS:
+                load_b(jc + 3)
+            for it in range(I_TILES):
+                product_and_norm(it, jc, b_codes, b_scales)

@@ -17,10 +17,14 @@ NI = 512
 NK = P * PACK
 NJ = 512
 ND = 8
+HALF = ND // 2
 I_TILES = NI // P
 JC = 128
 J_CHUNKS = NJ // JC
-HALF = ND // 2
+PAIR = 2
+I_PAIRS = I_TILES // PAIR
+BLOCK = PAIR * JC
+LOADS_AHEAD = 3
 EPS = 1e-5
 
 FLOPS = 2 * NI * NJ * NK * ND
@@ -35,18 +39,19 @@ def tile_trianglemultiplicativeupdate_pa_kernel(
     mik_rows = mask_ik.rearrange("b (n p) k -> p (b n) k", p=P)
     b_rows = b_gated.rearrange("b (t p) j d -> p (b t) (j d)", p=P)
     mkj_rows = mask_kj.rearrange("b (t p) j -> p (b t) j", p=P)
-    out_rows = out.rearrange("b (n p) j d -> (b n) p (j d)", p=P)
+    out_blocks = out.rearrange("b (n p) j d -> p (b n) (j d)", p=P)
 
     with ExitStack() as ctx:
         consts = ctx.enter_context(tc.tile_pool(name="consts", bufs=1))
         keep = ctx.enter_context(tc.tile_pool(name="keep", bufs=1))
-        a_in = ctx.enter_context(tc.tile_pool(name="a_in", bufs=3))
+        a_in = ctx.enter_context(tc.tile_pool(name="a_in", bufs=LOADS_AHEAD))
         a_work = ctx.enter_context(tc.tile_pool(name="a_work", bufs=2))
-        b_in = ctx.enter_context(tc.tile_pool(name="b_in", bufs=3))
+        b_in = ctx.enter_context(tc.tile_pool(name="b_in", bufs=LOADS_AHEAD))
         b_work = ctx.enter_context(tc.tile_pool(name="b_work", bufs=2))
-        b_mx = ctx.enter_context(tc.tile_pool(name="b_mx", bufs=3))
+        b_mx = ctx.enter_context(tc.tile_pool(name="b_mx", bufs=J_CHUNKS))
         ln = ctx.enter_context(tc.tile_pool(name="ln", bufs=3))
-        results = ctx.enter_context(tc.tile_pool(name="results", bufs=4))
+        planes = ctx.enter_context(tc.tile_pool(name="planes", bufs=2))
+        results = ctx.enter_context(tc.tile_pool(name="results", bufs=3))
         psum = ctx.enter_context(tc.psum_pool(name="psum", bufs=8))
 
         ident_f32 = consts.tile([P, P], F32)
@@ -64,12 +69,15 @@ def tile_trianglemultiplicativeupdate_pa_kernel(
         eps_col = consts.tile([P, 1], F32)
         nc.vector.memset(eps_col[:], EPS)
 
+        a_codes = keep.tile([P, I_TILES, ND * P], U32, align_bytes=64)
+        a_scales = keep.tile([P, I_TILES, ND * P], U8, align_bytes=64)
         mik = keep.tile([P, I_TILES, NK], BF16)
-        nc.sync.dma_start(out=mik[:], in_=mik_rows)
+        mikT = keep.tile([P, I_TILES, P, PACK], BF16)
         mkj = keep.tile([P, PACK, NJ], BF16)
-
+        mkj_grouped = keep.tile([P, NJ, PACK], BF16)
         a_raw_tiles = []
         b_raw_tiles = []
+        quantised_b = []
 
         def load_a(it):
             a_raw = a_in.tile([P, NK * ND], BF16)
@@ -81,16 +89,6 @@ def tile_trianglemultiplicativeupdate_pa_kernel(
             nc.sync.dma_start(out=b_raw[:], in_=b_rows[:, :, jc * JC * ND : (jc + 1) * JC * ND])
             b_raw_tiles.append(b_raw)
 
-        load_a(0)
-        load_a(1)
-        nc.sync.dma_start(out=mkj[:], in_=mkj_rows)
-        load_b(0)
-        load_a(2)
-
-        a_codes = keep.tile([P, I_TILES, ND * P], U32, align_bytes=64)
-        a_scales = keep.tile([P, I_TILES, ND * P], U8, align_bytes=64)
-        mikT = keep.tile([P, I_TILES, P, PACK], BF16)
-
         def prepare_a(it):
             a_raw = a_raw_tiles[it]
             maskT_ps = psum.tile([P, PACK, P], BF16, tag="bank")
@@ -98,16 +96,20 @@ def tile_trianglemultiplicativeupdate_pa_kernel(
                 nc.tensor.transpose(maskT_ps[:, t, :], mik[:, it, t * P : (t + 1) * P], ident_bf16[:])
             nc.vector.tensor_copy(out=mikT[:, it, :, :], in_=maskT_ps[:].rearrange("p t i -> p i t"))
 
-            a_words = a_raw[:].bitcast(F32).rearrange("p (k w) -> p k w", w=ND // 2)
+            a_words = a_raw[:].bitcast(F32).rearrange("p (k w) -> p k w", w=HALF)
             a_grouped = a_work.tile([P, ND, P, PACK], BF16, align_bytes=64)
-            for w in range(ND // 2):
+            for w in range(HALF):
                 aT_ps = psum.tile([P, PACK * P], F32, tag="bank")
                 for t in range(PACK):
-                    nc.tensor.transpose(aT_ps[:, t * P : (t + 1) * P], a_words[:, t * P : (t + 1) * P, w], ident_f32[:])
+                    nc.tensor.transpose(
+                        aT_ps[:, t * P : (t + 1) * P], a_words[:, t * P : (t + 1) * P, w], ident_f32[:]
+                    )
                 nc.scalar.copy(
                     out=a_grouped[:, 2 * w : 2 * w + 2, :, :],
                     in_=aT_ps[:].bitcast(BF16).rearrange("p (t i e) -> p e i t", t=PACK, e=2),
                 )
+            if it + LOADS_AHEAD < I_TILES:
+                load_a(it + LOADS_AHEAD)
             a_flat = a_grouped[:].rearrange("p d i t -> p d (i t)")
             nc.vector.tensor_tensor(
                 out=a_flat,
@@ -121,8 +123,6 @@ def tile_trianglemultiplicativeupdate_pa_kernel(
                 in_=a_grouped[:].rearrange("p d i t -> p (d i t)"),
             )
 
-        mkj_grouped = keep.tile([P, NJ, PACK], BF16)
-
         def prepare_b(jc):
             b_raw = b_raw_tiles[jc]
             b_grouped = b_work.tile([P, ND, JC, PACK], BF16, align_bytes=64)
@@ -131,6 +131,8 @@ def tile_trianglemultiplicativeupdate_pa_kernel(
             for h in range(2):
                 half = slice(h * HALF, (h + 1) * HALF)
                 nc.scalar.copy(out=dst[:, :, :, half], in_=src[:, :, :, half])
+            if jc + LOADS_AHEAD < J_CHUNKS:
+                load_b(jc + LOADS_AHEAD)
             b_flat = b_grouped[:].rearrange("p d j t -> p d (j t)")
             nc.vector.tensor_tensor(
                 out=b_flat,
@@ -148,53 +150,79 @@ def tile_trianglemultiplicativeupdate_pa_kernel(
                 scales=b_scales[:].rearrange("p d j -> p (d j)"),
                 in_=b_grouped[:].rearrange("p d j t -> p (d j t)"),
             )
-            return b_codes, b_scales
+            quantised_b.append((b_codes, b_scales))
 
-        def product_and_norm(it, jc, b_codes, b_scales):
-            sum_ps = psum.tile([P, JC], F32, tag="bank")
-            x_lo = psum.tile([P, HALF, JC], F32, tag="bank")
-            x_hi = psum.tile([P, HALF, JC], F32, tag="bank")
-            x_ps = [x_lo, x_hi]
-            for d in range(ND):
-                operands = dict(
-                    lhsT=a_codes[:, it, d * P : (d + 1) * P].bitcast(FP8X4),
-                    lhsT_scale=a_scales[:, it, d * P : (d + 1) * P],
-                    rhs=b_codes[:, d, :].bitcast(FP8X4),
-                    rhs_scale=b_scales[:, d, :],
-                )
-                nc.tensor.matmul_mx(out=x_ps[d // HALF][:, d % HALF, :], start=True, stop=True, **operands)
-                nc.tensor.matmul_mx(out=sum_ps[:], start=(d == 0), stop=(d == ND - 1), **operands)
+        def prepare_inputs(ip, jc):
+            if jc == 0:
+                for n in range(PAIR):
+                    prepare_a(ip * PAIR + n)
+            if ip == 0:
+                prepare_b(jc)
 
-            mean = ln.tile([P, JC], F32)
-            nc.scalar.activation(out=mean[:], in_=sum_ps[:], func=ACT.Copy, scale=1.0 / ND)
-            mean_sq = ln.tile([P, JC], F32)
+        def product(where, ip, jc, n, d, first, last):
+            it = ip * PAIR + n
+            b_codes, b_scales = quantised_b[jc]
+            nc.tensor.matmul_mx(
+                out=where[:, n * JC : (n + 1) * JC],
+                lhsT=a_codes[:, it, d * P : (d + 1) * P].bitcast(FP8X4),
+                lhsT_scale=a_scales[:, it, d * P : (d + 1) * P],
+                rhs=b_codes[:, d, :].bitcast(FP8X4),
+                rhs_scale=b_scales[:, d, :],
+                start=first,
+                stop=last,
+            )
+
+        def products_of_two_channels(ip, jc, q):
+            x_ps = psum.tile([P, 2, BLOCK], F32, tag="bank")
+            for e in range(2):
+                for n in range(PAIR):
+                    product(x_ps[:, e, :], ip, jc, n, 2 * q + e, True, True)
+            return x_ps
+
+        def statistics(ip, jc):
+            sum_ps = psum.tile([P, BLOCK], F32, tag="bank")
+            for n in range(PAIR):
+                for d in range(ND):
+                    product(sum_ps, ip, jc, n, d, d == 0, d == ND - 1)
+            mean_sq = ln.tile([P, BLOCK], F32)
             nc.scalar.activation(out=mean_sq[:], in_=sum_ps[:], func=ACT.Square, scale=1.0 / ND)
-            squares = ln.tile([P, ND, JC], F32)
-            for h in range(2):
-                nc.scalar.activation(
-                    out=squares[:, h * HALF : (h + 1) * HALF, :], in_=x_ps[h][:], func=ACT.Square
-                )
-            sum4 = ln.tile([P, 4, JC], F32)
-            nc.gpsimd.tensor_tensor(out=sum4[:], in0=squares[:, 0:4, :], in1=squares[:, 4:8, :], op=ALU.add)
-            sum2 = ln.tile([P, 2, JC], F32)
-            nc.gpsimd.tensor_tensor(out=sum2[:], in0=sum4[:, 0:2, :], in1=sum4[:, 2:4, :], op=ALU.add)
-            sum1 = ln.tile([P, JC], F32)
-            nc.gpsimd.tensor_tensor(out=sum1[:], in0=sum2[:, 0, :], in1=sum2[:, 1, :], op=ALU.add)
 
-            var = ln.tile([P, JC], F32)
+            squares = planes.tile([P, ND, BLOCK], F32)
+            for q in range(HALF):
+                x_ps = products_of_two_channels(ip, jc, q)
+                nc.scalar.activation(out=squares[:, 2 * q : 2 * q + 2, :], in_=x_ps[:], func=ACT.Square)
+
+            sum_sq_T_ps = psum.tile([P, BLOCK], F32, tag="bank")
+            for n in range(PAIR):
+                cols = slice(n * JC, (n + 1) * JC)
+                for d in range(ND):
+                    nc.tensor.matmul(
+                        out=sum_sq_T_ps[:, cols],
+                        lhsT=squares[:, d, cols],
+                        rhs=ident_f32[:],
+                        is_transpose=True,
+                        start=(d == 0),
+                        stop=(d == ND - 1),
+                    )
+            sum_sq_T = ln.tile([P, BLOCK], F32)
+            nc.scalar.copy(out=sum_sq_T[:], in_=sum_sq_T_ps[:])
+            sum_sq_ps = psum.tile([P, BLOCK], F32, tag="bank")
+            for n in range(PAIR):
+                cols = slice(n * JC, (n + 1) * JC)
+                nc.tensor.transpose(sum_sq_ps[:, cols], sum_sq_T[:, cols], ident_f32[:])
+
+            var = ln.tile([P, BLOCK], F32)
             nc.vector.scalar_tensor_tensor(
-                out=var[:], in0=sum1[:], scalar=1.0 / ND, in1=mean_sq[:], op0=ALU.mult, op1=ALU.subtract
+                out=var[:], in0=sum_sq_ps[:], scalar=1.0 / ND, in1=mean_sq[:], op0=ALU.mult, op1=ALU.subtract
             )
-            rstd = ln.tile([P, JC], F32)
+            rstd = ln.tile([P, BLOCK], F32)
             nc.scalar.activation(out=rstd[:], in_=var[:], func=ACT.Abs_reciprocal_sqrt, bias=eps_col[:, 0:1])
-            neg_mean_rstd = ln.tile([P, JC], F32)
+            neg_mean_rstd = ln.tile([P, BLOCK], F32)
             nc.vector.scalar_tensor_tensor(
-                out=neg_mean_rstd[:], in0=mean[:], scalar=-1.0, in1=rstd[:], op0=ALU.mult, op1=ALU.mult
+                out=neg_mean_rstd[:], in0=sum_ps[:], scalar=-1.0 / ND, in1=rstd[:], op0=ALU.mult, op1=ALU.mult
             )
-
-            shift = ln.tile([P, ND, JC], F32)
-            scaled = ln.tile([P, ND, JC], F32)
-            for d in range(ND):
+            shift = planes.tile([P, ND, BLOCK], F32)
+            for d in range(HALF):
                 nc.scalar.activation(
                     out=shift[:, d, :],
                     in_=neg_mean_rstd[:],
@@ -202,39 +230,60 @@ def tile_trianglemultiplicativeupdate_pa_kernel(
                     scale=w_col[:, d : d + 1],
                     bias=bias_col[:, d : d + 1],
                 )
-                nc.vector.scalar_tensor_tensor(
-                    out=scaled[:, d, :],
-                    in0=x_ps[d // HALF][:, d % HALF, :],
-                    scalar=w_col[:, d : d + 1],
-                    in1=rstd[:],
+            for d in range(HALF, ND):
+                nc.vector.tensor_scalar(
+                    out=shift[:, d, :],
+                    in0=neg_mean_rstd[:],
+                    scalar1=w_col[:, d : d + 1],
+                    scalar2=bias_col[:, d : d + 1],
                     op0=ALU.mult,
-                    op1=ALU.mult,
+                    op1=ALU.add,
                 )
-            result = results.tile([P, JC, ND], F32)
-            for h in range(2):
-                half = slice(h * HALF, (h + 1) * HALF)
-                nc.vector.tensor_tensor(
-                    out=result[:, :, half],
-                    in0=scaled[:, half, :].rearrange("p d j -> p j d"),
-                    in1=shift[:, half, :].rearrange("p d j -> p j d"),
-                    op=ALU.add,
-                )
+            return rstd, shift
+
+        def normalise(ip, jc, rstd, shift):
+            scaled = planes.tile([P, ND, BLOCK], F32)
+            for q in range(HALF):
+                x_ps = products_of_two_channels(ip, jc, q)
+                for e in range(2):
+                    d = 2 * q + e
+                    nc.vector.scalar_tensor_tensor(
+                        out=scaled[:, d, :],
+                        in0=x_ps[:, e, :],
+                        scalar=w_col[:, d : d + 1],
+                        in1=rstd[:],
+                        op0=ALU.mult,
+                        op1=ALU.mult,
+                    )
+            result = results.tile([P, BLOCK, ND], F32)
+            nc.vector.tensor_tensor(
+                out=result[:].rearrange("p (c e) d -> p c d e", e=2),
+                in0=scaled[:].rearrange("p d (c e) -> p c d e", e=2),
+                in1=shift[:].rearrange("p d (c e) -> p c d e", e=2),
+                op=ALU.add,
+            )
             nc.sync.dma_start(
-                out=out_rows[it, :, jc * JC * ND : (jc + 1) * JC * ND],
-                in_=result[:].rearrange("p j d -> p (j d)"),
+                out=out_blocks[:, ip * PAIR : (ip + 1) * PAIR, jc * JC * ND : (jc + 1) * JC * ND],
+                in_=result[:].rearrange("p (n j) d -> p n (j d)", n=PAIR),
             )
 
-        prepare_a(0)
-        load_a(3)
-        prepare_a(1)
-        load_b(1)
+        nc.sync.dma_start(out=mik[:], in_=mik_rows)
+        load_a(0)
+        load_a(1)
+        nc.sync.dma_start(out=mkj[:], in_=mkj_rows)
+        for jc in range(LOADS_AHEAD):
+            load_b(jc)
+        load_a(2)
         nc.vector.tensor_copy(out=mkj_grouped[:], in_=mkj[:].rearrange("p t j -> p j t"))
-        prepare_a(2)
-        load_b(2)
-        prepare_a(3)
-        for jc in range(J_CHUNKS):
-            b_codes, b_scales = prepare_b(jc)
-            if jc + 3 < J_CHUNKS:
-                load_b(jc + 3)
-            for it in range(I_TILES):
-                product_and_norm(it, jc, b_codes, b_scales)
+
+        blocks = [(ip, jc) for ip in range(I_PAIRS) for jc in range(J_CHUNKS)]
+        stats = []
+        prepare_inputs(*blocks[0])
+        prepare_inputs(*blocks[1])
+        stats.append(statistics(*blocks[0]))
+        for n in range(len(blocks)):
+            if n + 2 < len(blocks):
+                prepare_inputs(*blocks[n + 2])
+            if n + 1 < len(blocks):
+                stats.append(statistics(*blocks[n + 1]))
+            normalise(*blocks[n], *stats[n])

@@ -42,16 +42,16 @@ def tile_trianglemultiplicativeupdate_pa_kernel(
     out_blocks = out.rearrange("b (n p) j d -> p (b n) (j d)", p=P)
 
     with ExitStack() as ctx:
+        ctx.enter_context(tc.manual_schedule())
         consts = ctx.enter_context(tc.tile_pool(name="consts", bufs=1))
         keep = ctx.enter_context(tc.tile_pool(name="keep", bufs=1))
         a_in = ctx.enter_context(tc.tile_pool(name="a_in", bufs=LOADS_AHEAD))
         a_work = ctx.enter_context(tc.tile_pool(name="a_work", bufs=2))
         b_in = ctx.enter_context(tc.tile_pool(name="b_in", bufs=LOADS_AHEAD))
-        b_work = ctx.enter_context(tc.tile_pool(name="b_work", bufs=2))
+        b_work = ctx.enter_context(tc.tile_pool(name="b_work", bufs=3))
         b_mx = ctx.enter_context(tc.tile_pool(name="b_mx", bufs=J_CHUNKS))
-        ln = ctx.enter_context(tc.tile_pool(name="ln", bufs=3))
+        ln = ctx.enter_context(tc.tile_pool(name="ln", bufs=4))
         planes = ctx.enter_context(tc.tile_pool(name="planes", bufs=2))
-        results = ctx.enter_context(tc.tile_pool(name="results", bufs=3))
         psum = ctx.enter_context(tc.psum_pool(name="psum", bufs=8))
 
         ident_f32 = consts.tile([P, P], F32)
@@ -59,15 +59,13 @@ def tile_trianglemultiplicativeupdate_pa_kernel(
         ident_bf16 = consts.tile([P, P], BF16)
         make_identity(nc, ident_bf16[:])
         w_bf16 = consts.tile([P, ND], BF16)
-        nc.scalar.dma_start(out=w_bf16[:], in_=ln_out_w.partition_broadcast(P))
+        nc.gpsimd.dma_start(out=w_bf16[:], in_=ln_out_w.partition_broadcast(P))
         bias_bf16 = consts.tile([P, ND], BF16)
-        nc.scalar.dma_start(out=bias_bf16[:], in_=ln_out_b.partition_broadcast(P))
-        w_col = consts.tile([P, ND], F32)
-        nc.vector.tensor_copy(out=w_col[:], in_=w_bf16[:])
-        bias_col = consts.tile([P, ND], F32)
-        nc.vector.tensor_copy(out=bias_col[:], in_=bias_bf16[:])
+        nc.gpsimd.dma_start(out=bias_bf16[:], in_=ln_out_b.partition_broadcast(P))
         eps_col = consts.tile([P, 1], F32)
         nc.vector.memset(eps_col[:], EPS)
+        w_col = consts.tile([P, ND], F32)
+        bias_col = consts.tile([P, ND], F32)
 
         a_codes = keep.tile([P, I_TILES, ND * P], U32, align_bytes=64)
         a_scales = keep.tile([P, I_TILES, ND * P], U8, align_bytes=64)
@@ -76,7 +74,9 @@ def tile_trianglemultiplicativeupdate_pa_kernel(
         mkj = keep.tile([P, PACK, NJ], BF16)
         mkj_grouped = keep.tile([P, NJ, PACK], BF16)
         a_raw_tiles = []
+        a_grouped_tiles = []
         b_raw_tiles = []
+        b_grouped_tiles = []
         quantised_b = []
 
         def load_a(it):
@@ -89,7 +89,7 @@ def tile_trianglemultiplicativeupdate_pa_kernel(
             nc.sync.dma_start(out=b_raw[:], in_=b_rows[:, :, jc * JC * ND : (jc + 1) * JC * ND])
             b_raw_tiles.append(b_raw)
 
-        def prepare_a(it):
+        def transpose_a(it):
             a_raw = a_raw_tiles[it]
             maskT_ps = psum.tile([P, PACK, P], BF16, tag="bank")
             for t in range(PACK):
@@ -98,32 +98,45 @@ def tile_trianglemultiplicativeupdate_pa_kernel(
 
             a_words = a_raw[:].bitcast(F32).rearrange("p (k w) -> p k w", w=HALF)
             a_grouped = a_work.tile([P, ND, P, PACK], BF16, align_bytes=64)
+            a_grouped_tiles.append(a_grouped)
+            pair_mask = mikT[:, it, :, :].unsqueeze(1).to_broadcast([P, 2, P, PACK])
             for w in range(HALF):
                 aT_ps = psum.tile([P, PACK * P], F32, tag="bank")
                 for t in range(PACK):
                     nc.tensor.transpose(
                         aT_ps[:, t * P : (t + 1) * P], a_words[:, t * P : (t + 1) * P, w], ident_f32[:]
                     )
-                nc.scalar.copy(
-                    out=a_grouped[:, 2 * w : 2 * w + 2, :, :],
-                    in_=aT_ps[:].bitcast(BF16).rearrange("p (t i e) -> p e i t", t=PACK, e=2),
-                )
-            if it + LOADS_AHEAD < I_TILES:
-                load_a(it + LOADS_AHEAD)
-            a_flat = a_grouped[:].rearrange("p d i t -> p d (i t)")
-            nc.vector.tensor_tensor(
-                out=a_flat,
-                in0=a_flat,
-                in1=mikT[:, it, :, :].rearrange("p i t -> p (i t)").unsqueeze(1).to_broadcast([P, ND, P * PACK]),
-                op=ALU.mult,
-            )
+                pair = a_grouped[:, 2 * w : 2 * w + 2, :, :]
+                pair_T = aT_ps[:].bitcast(BF16).rearrange("p (t i e) -> p e i t", t=PACK, e=2)
+                if w == 0:
+                    nc.scalar.copy(out=pair, in_=pair_T)
+                else:
+                    nc.vector.tensor_tensor(out=pair, in0=pair_T, in1=pair_mask, op=ALU.mult)
+
+        def mask_first_pair_of_a(it):
+            pair = a_grouped_tiles[it][:, 0:2, :, :]
+            pair_mask = mikT[:, it, :, :].unsqueeze(1).to_broadcast([P, 2, P, PACK])
+            nc.vector.tensor_tensor(out=pair, in0=pair, in1=pair_mask, op=ALU.mult)
+
+        def quantise_a(it):
             nc.vector.quantize_mx(
                 out=a_codes[:, it, :].bitcast(FP8X4),
                 scales=a_scales[:, it, :],
-                in_=a_grouped[:].rearrange("p d i t -> p (d i t)"),
+                in_=a_grouped_tiles[it][:].rearrange("p d i t -> p (d i t)"),
             )
 
-        def prepare_b(jc):
+        def prepare_a_pair(ip):
+            tiles = range(ip * PAIR, (ip + 1) * PAIR)
+            for it in tiles:
+                transpose_a(it)
+                if it + LOADS_AHEAD < I_TILES:
+                    load_a(it + LOADS_AHEAD)
+            for it in tiles:
+                mask_first_pair_of_a(it)
+            for it in tiles:
+                quantise_a(it)
+
+        def regroup_b(jc):
             b_raw = b_raw_tiles[jc]
             b_grouped = b_work.tile([P, ND, JC, PACK], BF16, align_bytes=64)
             src = b_raw[:].rearrange("p t (j d) -> p j t d", d=ND)
@@ -131,8 +144,12 @@ def tile_trianglemultiplicativeupdate_pa_kernel(
             for h in range(2):
                 half = slice(h * HALF, (h + 1) * HALF)
                 nc.scalar.copy(out=dst[:, :, :, half], in_=src[:, :, :, half])
+            b_grouped_tiles.append(b_grouped)
             if jc + LOADS_AHEAD < J_CHUNKS:
                 load_b(jc + LOADS_AHEAD)
+
+        def quantise_b(jc):
+            b_grouped = b_grouped_tiles[jc]
             b_flat = b_grouped[:].rearrange("p d j t -> p d (j t)")
             nc.vector.tensor_tensor(
                 out=b_flat,
@@ -152,14 +169,11 @@ def tile_trianglemultiplicativeupdate_pa_kernel(
             )
             quantised_b.append((b_codes, b_scales))
 
-        def prepare_inputs(ip, jc):
-            if jc == 0:
-                for n in range(PAIR):
-                    prepare_a(ip * PAIR + n)
-            if ip == 0:
-                prepare_b(jc)
+        blocks = [(ip, jc) for jc in range(J_CHUNKS) for ip in range(I_PAIRS)]
+        tiles_of = [dict() for block in blocks]
 
-        def product(where, ip, jc, n, d, first, last):
+        def product(where, block, n, d, first, last):
+            ip, jc = block
             it = ip * PAIR + n
             b_codes, b_scales = quantised_b[jc]
             nc.tensor.matmul_mx(
@@ -172,26 +186,30 @@ def tile_trianglemultiplicativeupdate_pa_kernel(
                 stop=last,
             )
 
-        def products_of_two_channels(ip, jc, q):
+        def products_of_two_channels(block, q):
             x_ps = psum.tile([P, 2, BLOCK], F32, tag="bank")
             for e in range(2):
                 for n in range(PAIR):
-                    product(x_ps[:, e, :], ip, jc, n, 2 * q + e, True, True)
+                    product(x_ps[:, e, :], block, n, 2 * q + e, True, True)
             return x_ps
 
-        def statistics(ip, jc):
+        def sums_and_squares(m):
             sum_ps = psum.tile([P, BLOCK], F32, tag="bank")
             for n in range(PAIR):
                 for d in range(ND):
-                    product(sum_ps, ip, jc, n, d, d == 0, d == ND - 1)
+                    product(sum_ps, blocks[m], n, d, d == 0, d == ND - 1)
             mean_sq = ln.tile([P, BLOCK], F32)
             nc.scalar.activation(out=mean_sq[:], in_=sum_ps[:], func=ACT.Square, scale=1.0 / ND)
-
+            neg_mean = ln.tile([P, BLOCK], F32)
+            nc.scalar.activation(out=neg_mean[:], in_=sum_ps[:], func=ACT.Copy, scale=-1.0 / ND)
             squares = planes.tile([P, ND, BLOCK], F32)
             for q in range(HALF):
-                x_ps = products_of_two_channels(ip, jc, q)
+                x_ps = products_of_two_channels(blocks[m], q)
                 nc.scalar.activation(out=squares[:, 2 * q : 2 * q + 2, :], in_=x_ps[:], func=ACT.Square)
+            tiles_of[m].update(mean_sq=mean_sq, neg_mean=neg_mean, squares=squares)
 
+        def add_squares(m):
+            squares = tiles_of[m]["squares"]
             sum_sq_T_ps = psum.tile([P, BLOCK], F32, tag="bank")
             for n in range(PAIR):
                 cols = slice(n * JC, (n + 1) * JC)
@@ -204,62 +222,82 @@ def tile_trianglemultiplicativeupdate_pa_kernel(
                         start=(d == 0),
                         stop=(d == ND - 1),
                     )
+            tiles_of[m].update(sum_sq_T_ps=sum_sq_T_ps)
+
+        def copy_sum_of_squares(m):
             sum_sq_T = ln.tile([P, BLOCK], F32)
-            nc.scalar.copy(out=sum_sq_T[:], in_=sum_sq_T_ps[:])
+            nc.scalar.copy(out=sum_sq_T[:], in_=tiles_of[m]["sum_sq_T_ps"][:])
+            tiles_of[m].update(sum_sq_T=sum_sq_T)
+
+        def transpose_sum_of_squares_back(m):
+            sum_sq_T = tiles_of[m]["sum_sq_T"]
             sum_sq_ps = psum.tile([P, BLOCK], F32, tag="bank")
             for n in range(PAIR):
                 cols = slice(n * JC, (n + 1) * JC)
                 nc.tensor.transpose(sum_sq_ps[:, cols], sum_sq_T[:, cols], ident_f32[:])
+            tiles_of[m].update(sum_sq_ps=sum_sq_ps)
 
+        def variance(m):
             var = ln.tile([P, BLOCK], F32)
             nc.vector.scalar_tensor_tensor(
-                out=var[:], in0=sum_sq_ps[:], scalar=1.0 / ND, in1=mean_sq[:], op0=ALU.mult, op1=ALU.subtract
+                out=var[:],
+                in0=tiles_of[m]["sum_sq_ps"][:],
+                scalar=1.0 / ND,
+                in1=tiles_of[m]["mean_sq"][:],
+                op0=ALU.mult,
+                op1=ALU.subtract,
             )
+            tiles_of[m].update(var=var)
+
+        def reciprocal_std(m):
             rstd = ln.tile([P, BLOCK], F32)
-            nc.scalar.activation(out=rstd[:], in_=var[:], func=ACT.Abs_reciprocal_sqrt, bias=eps_col[:, 0:1])
-            neg_mean_rstd = ln.tile([P, BLOCK], F32)
-            nc.vector.scalar_tensor_tensor(
-                out=neg_mean_rstd[:], in0=sum_ps[:], scalar=-1.0 / ND, in1=rstd[:], op0=ALU.mult, op1=ALU.mult
+            nc.scalar.activation(
+                out=rstd[:], in_=tiles_of[m]["var"][:], func=ACT.Abs_reciprocal_sqrt, bias=eps_col[:, 0:1]
             )
+            tiles_of[m].update(rstd=rstd)
+
+        def minus_mean_times_rstd(m):
+            neg_mean_rstd = ln.tile([P, BLOCK], F32)
+            nc.vector.tensor_tensor(
+                out=neg_mean_rstd[:], in0=tiles_of[m]["neg_mean"][:], in1=tiles_of[m]["rstd"][:], op=ALU.mult
+            )
+            tiles_of[m].update(neg_mean_rstd=neg_mean_rstd)
+
+        def shifts(m):
             shift = planes.tile([P, ND, BLOCK], F32)
-            for d in range(HALF):
+            for d in range(ND):
                 nc.scalar.activation(
                     out=shift[:, d, :],
-                    in_=neg_mean_rstd[:],
+                    in_=tiles_of[m]["neg_mean_rstd"][:],
                     func=ACT.Identity,
                     scale=w_col[:, d : d + 1],
                     bias=bias_col[:, d : d + 1],
                 )
-            for d in range(HALF, ND):
-                nc.vector.tensor_scalar(
-                    out=shift[:, d, :],
-                    in0=neg_mean_rstd[:],
-                    scalar1=w_col[:, d : d + 1],
-                    scalar2=bias_col[:, d : d + 1],
-                    op0=ALU.mult,
-                    op1=ALU.add,
-                )
-            return rstd, shift
+            tiles_of[m].update(shift=shift)
 
-        def normalise(ip, jc, rstd, shift):
-            scaled = planes.tile([P, ND, BLOCK], F32)
+        def scale_products(m):
+            scaled = planes.tile([P, ND, BLOCK], F32, bufs=1)
             for q in range(HALF):
-                x_ps = products_of_two_channels(ip, jc, q)
+                x_ps = products_of_two_channels(blocks[m], q)
                 for e in range(2):
                     d = 2 * q + e
                     nc.vector.scalar_tensor_tensor(
                         out=scaled[:, d, :],
                         in0=x_ps[:, e, :],
                         scalar=w_col[:, d : d + 1],
-                        in1=rstd[:],
+                        in1=tiles_of[m]["rstd"][:],
                         op0=ALU.mult,
                         op1=ALU.mult,
                     )
-            result = results.tile([P, BLOCK, ND], F32)
+            tiles_of[m].update(scaled=scaled)
+
+        def add_shifts_and_store(m):
+            ip, jc = blocks[m]
+            result = planes.tile([P, BLOCK, ND], F32)
             nc.vector.tensor_tensor(
                 out=result[:].rearrange("p (c e) d -> p c d e", e=2),
-                in0=scaled[:].rearrange("p d (c e) -> p c d e", e=2),
-                in1=shift[:].rearrange("p d (c e) -> p c d e", e=2),
+                in0=tiles_of[m]["scaled"][:].rearrange("p d (c e) -> p c d e", e=2),
+                in1=tiles_of[m]["shift"][:].rearrange("p d (c e) -> p c d e", e=2),
                 op=ALU.add,
             )
             nc.sync.dma_start(
@@ -271,19 +309,34 @@ def tile_trianglemultiplicativeupdate_pa_kernel(
         load_a(0)
         load_a(1)
         nc.sync.dma_start(out=mkj[:], in_=mkj_rows)
-        for jc in range(LOADS_AHEAD):
-            load_b(jc)
+        load_b(0)
         load_a(2)
-        nc.vector.tensor_copy(out=mkj_grouped[:], in_=mkj[:].rearrange("p t j -> p j t"))
+        load_b(1)
+        load_b(2)
 
-        blocks = [(ip, jc) for ip in range(I_PAIRS) for jc in range(J_CHUNKS)]
-        stats = []
-        prepare_inputs(*blocks[0])
-        prepare_inputs(*blocks[1])
-        stats.append(statistics(*blocks[0]))
-        for n in range(len(blocks)):
-            if n + 2 < len(blocks):
-                prepare_inputs(*blocks[n + 2])
-            if n + 1 < len(blocks):
-                stats.append(statistics(*blocks[n + 1]))
-            normalise(*blocks[n], *stats[n])
+        prepare_a_pair(0)
+        nc.scalar.copy(out=mkj_grouped[:], in_=mkj[:].rearrange("p t j -> p j t"))
+        regroup_b(0)
+        quantise_b(0)
+        prepare_a_pair(1)
+        for jc in range(1, J_CHUNKS):
+            regroup_b(jc)
+            quantise_b(jc)
+        nc.vector.tensor_copy(out=w_col[:], in_=w_bf16[:])
+        nc.vector.tensor_copy(out=bias_col[:], in_=bias_bf16[:])
+
+        def stage(work, m):
+            if 0 <= m < len(blocks):
+                work(m)
+
+        for m in range(-4, len(blocks)):
+            stage(scale_products, m)
+            stage(add_squares, m + 2)
+            stage(copy_sum_of_squares, m + 2)
+            stage(minus_mean_times_rstd, m + 1)
+            stage(add_shifts_and_store, m)
+            stage(sums_and_squares, m + 4)
+            stage(transpose_sum_of_squares_back, m + 2)
+            stage(variance, m + 2)
+            stage(reciprocal_std, m + 2)
+            stage(shifts, m + 1)

@@ -39,7 +39,7 @@ def tile_trianglemultiplicativeupdate_pa_kernel(
     mik_rows = mask_ik.rearrange("b (n p) k -> p (b n) k", p=P)
     b_rows = b_gated.rearrange("b (t p) j d -> p (b t) (j d)", p=P)
     mkj_rows = mask_kj.rearrange("b (t p) j -> p (b t) j", p=P)
-    out_blocks = out.rearrange("b (n p) j d -> p (b n) (j d)", p=P)
+    out_rows = out.rearrange("b (n p) j d -> (b n) p (j d)", p=P)
 
     with ExitStack() as ctx:
         ctx.enter_context(tc.manual_schedule())
@@ -52,6 +52,7 @@ def tile_trianglemultiplicativeupdate_pa_kernel(
         b_mx = ctx.enter_context(tc.tile_pool(name="b_mx", bufs=J_CHUNKS))
         ln = ctx.enter_context(tc.tile_pool(name="ln", bufs=4))
         planes = ctx.enter_context(tc.tile_pool(name="planes", bufs=2))
+        results = ctx.enter_context(tc.tile_pool(name="results", bufs=4))
         psum = ctx.enter_context(tc.psum_pool(name="psum", bufs=8))
 
         ident_f32 = consts.tile([P, P], F32)
@@ -80,6 +81,7 @@ def tile_trianglemultiplicativeupdate_pa_kernel(
         quantised_b = []
 
         def load_a(it):
+            nc.sync.dma_start(out=mik[:, it, :], in_=mik_rows[:, it, :])
             a_raw = a_in.tile([P, NK * ND], BF16)
             nc.sync.dma_start(out=a_raw[:], in_=a_rows[it])
             a_raw_tiles.append(a_raw)
@@ -94,7 +96,7 @@ def tile_trianglemultiplicativeupdate_pa_kernel(
             maskT_ps = psum.tile([P, PACK, P], BF16, tag="bank")
             for t in range(PACK):
                 nc.tensor.transpose(maskT_ps[:, t, :], mik[:, it, t * P : (t + 1) * P], ident_bf16[:])
-            nc.vector.tensor_copy(out=mikT[:, it, :, :], in_=maskT_ps[:].rearrange("p t i -> p i t"))
+            nc.scalar.copy(out=mikT[:, it, :, :], in_=maskT_ps[:].rearrange("p t i -> p i t"))
 
             a_words = a_raw[:].bitcast(F32).rearrange("p (k w) -> p k w", w=HALF)
             a_grouped = a_work.tile([P, ND, P, PACK], BF16, align_bytes=64)
@@ -258,7 +260,7 @@ def tile_trianglemultiplicativeupdate_pa_kernel(
 
         def minus_mean_times_rstd(m):
             neg_mean_rstd = ln.tile([P, BLOCK], F32)
-            nc.vector.tensor_tensor(
+            nc.gpsimd.tensor_tensor(
                 out=neg_mean_rstd[:], in0=tiles_of[m]["neg_mean"][:], in1=tiles_of[m]["rstd"][:], op=ALU.mult
             )
             tiles_of[m].update(neg_mean_rstd=neg_mean_rstd)
@@ -266,12 +268,13 @@ def tile_trianglemultiplicativeupdate_pa_kernel(
         def shifts(m):
             shift = planes.tile([P, ND, BLOCK], F32)
             for d in range(ND):
-                nc.scalar.activation(
+                nc.gpsimd.tensor_scalar(
                     out=shift[:, d, :],
-                    in_=tiles_of[m]["neg_mean_rstd"][:],
-                    func=ACT.Identity,
-                    scale=w_col[:, d : d + 1],
-                    bias=bias_col[:, d : d + 1],
+                    in0=tiles_of[m]["neg_mean_rstd"][:],
+                    scalar1=w_col[:, d : d + 1],
+                    scalar2=bias_col[:, d : d + 1],
+                    op0=ALU.mult,
+                    op1=ALU.add,
                 )
             tiles_of[m].update(shift=shift)
 
@@ -293,19 +296,20 @@ def tile_trianglemultiplicativeupdate_pa_kernel(
 
         def add_shifts_and_store(m):
             ip, jc = blocks[m]
-            result = planes.tile([P, BLOCK, ND], F32)
-            nc.vector.tensor_tensor(
-                out=result[:].rearrange("p (c e) d -> p c d e", e=2),
-                in0=tiles_of[m]["scaled"][:].rearrange("p d (c e) -> p c d e", e=2),
-                in1=tiles_of[m]["shift"][:].rearrange("p d (c e) -> p c d e", e=2),
-                op=ALU.add,
-            )
-            nc.sync.dma_start(
-                out=out_blocks[:, ip * PAIR : (ip + 1) * PAIR, jc * JC * ND : (jc + 1) * JC * ND],
-                in_=result[:].rearrange("p (n j) d -> p n (j d)", n=PAIR),
-            )
+            for n in range(PAIR):
+                cols = slice(n * JC, (n + 1) * JC)
+                result = results.tile([P, JC, ND], F32)
+                nc.vector.tensor_tensor(
+                    out=result[:].rearrange("p (c e) d -> p c d e", e=2),
+                    in0=tiles_of[m]["scaled"][:, :, cols].rearrange("p d (c e) -> p c d e", e=2),
+                    in1=tiles_of[m]["shift"][:, :, cols].rearrange("p d (c e) -> p c d e", e=2),
+                    op=ALU.add,
+                )
+                nc.sync.dma_start(
+                    out=out_rows[ip * PAIR + n, :, jc * JC * ND : (jc + 1) * JC * ND],
+                    in_=result[:].rearrange("p j d -> p (j d)"),
+                )
 
-        nc.sync.dma_start(out=mik[:], in_=mik_rows)
         load_a(0)
         load_a(1)
         nc.sync.dma_start(out=mkj[:], in_=mkj_rows)

@@ -260,15 +260,23 @@ def tile_trianglemultiplicativeupdate_pa_kernel(
 
         def minus_mean_times_rstd(m):
             neg_mean_rstd = ln.tile([P, BLOCK], F32)
-            nc.gpsimd.tensor_tensor(
+            nc.vector.tensor_tensor(
                 out=neg_mean_rstd[:], in0=tiles_of[m]["neg_mean"][:], in1=tiles_of[m]["rstd"][:], op=ALU.mult
             )
             tiles_of[m].update(neg_mean_rstd=neg_mean_rstd)
 
         def shifts(m):
             shift = planes.tile([P, ND, BLOCK], F32)
-            for d in range(ND):
-                nc.gpsimd.tensor_scalar(
+            for d in range(HALF):
+                nc.scalar.activation(
+                    out=shift[:, d, :],
+                    in_=tiles_of[m]["neg_mean_rstd"][:],
+                    func=ACT.Identity,
+                    scale=w_col[:, d : d + 1],
+                    bias=bias_col[:, d : d + 1],
+                )
+            for d in range(HALF, ND):
+                nc.vector.tensor_scalar(
                     out=shift[:, d, :],
                     in0=tiles_of[m]["neg_mean_rstd"][:],
                     scalar1=w_col[:, d : d + 1],

from contextlib import ExitStack

import concourse.mybir as mybir
from concourse.masks import make_identity

FP8X4 = mybir.dt.float8_e4m3fn_x4
BF16 = mybir.dt.bfloat16
F32 = mybir.dt.float32
U32 = mybir.dt.uint32
U8 = mybir.dt.uint8
ALU = mybir.AluOpType
ACT = mybir.ActivationFunctionType

P = 128
PACK = 4
NI = 512
NK = P * PACK
NJ = 512
ND = 8
HALF = ND // 2
I_TILES = NI // P
JC = 128
J_CHUNKS = NJ // JC
PAIR = 2
I_PAIRS = I_TILES // PAIR
BLOCK = PAIR * JC
LOADS_AHEAD = 3
EPS = 1e-5

FLOPS = 2 * NI * NJ * NK * ND


def tile_trianglemultiplicativeupdate_pa_kernel(
    tc, a_gated, b_gated, mask_ik, mask_kj, ln_out_w, ln_out_b, out
):
    nc = tc.nc

    a_rows = a_gated.rearrange("b (n p) k d -> (b n) p (k d)", p=P)
    mik_rows = mask_ik.rearrange("b (n p) k -> p (b n) k", p=P)
    b_rows = b_gated.rearrange("b (t p) j d -> p (b t) (j d)", p=P)
    mkj_rows = mask_kj.rearrange("b (t p) j -> p (b t) j", p=P)
    out_rows = out.rearrange("b (n p) j d -> (b n) p (j d)", p=P)

    with ExitStack() as ctx:
        ctx.enter_context(tc.manual_schedule())
        consts = ctx.enter_context(tc.tile_pool(name="consts", bufs=1))
        keep = ctx.enter_context(tc.tile_pool(name="keep", bufs=1))
        a_in = ctx.enter_context(tc.tile_pool(name="a_in", bufs=LOADS_AHEAD))
        a_work = ctx.enter_context(tc.tile_pool(name="a_work", bufs=2))
        b_in = ctx.enter_context(tc.tile_pool(name="b_in", bufs=LOADS_AHEAD))
        b_work = ctx.enter_context(tc.tile_pool(name="b_work", bufs=3))
        b_mx = ctx.enter_context(tc.tile_pool(name="b_mx", bufs=J_CHUNKS))
        ln = ctx.enter_context(tc.tile_pool(name="ln", bufs=4))
        planes = ctx.enter_context(tc.tile_pool(name="planes", bufs=2))
        results = ctx.enter_context(tc.tile_pool(name="results", bufs=4))
        psum = ctx.enter_context(tc.psum_pool(name="psum", bufs=8))

        ident_f32 = consts.tile([P, P], F32)
        make_identity(nc, ident_f32[:])
        ident_bf16 = consts.tile([P, P], BF16)
        make_identity(nc, ident_bf16[:])
        w_bf16 = consts.tile([P, ND], BF16)
        nc.gpsimd.dma_start(out=w_bf16[:], in_=ln_out_w.partition_broadcast(P))
        bias_bf16 = consts.tile([P, ND], BF16)
        nc.gpsimd.dma_start(out=bias_bf16[:], in_=ln_out_b.partition_broadcast(P))
        eps_col = consts.tile([P, 1], F32)
        nc.vector.memset(eps_col[:], EPS)
        w_col = consts.tile([P, ND], F32)
        bias_col = consts.tile([P, ND], F32)

        a_codes = keep.tile([P, I_TILES, ND * P], U32, align_bytes=64)
        a_scales = keep.tile([P, I_TILES, ND * P], U8, align_bytes=64)
        mik = keep.tile([P, I_TILES, NK], BF16)
        mikT = keep.tile([P, I_TILES, P, PACK], BF16)
        mkj = keep.tile([P, PACK, NJ], BF16)
        mkj_grouped = keep.tile([P, NJ, PACK], BF16)
        a_raw_tiles = []
        a_grouped_tiles = []
        b_raw_tiles = []
        b_grouped_tiles = []
        quantised_b = []

        def load_a(it):
            nc.sync.dma_start(out=mik[:, it, :], in_=mik_rows[:, it, :])
            a_raw = a_in.tile([P, NK * ND], BF16)
            nc.sync.dma_start(out=a_raw[:], in_=a_rows[it])
            a_raw_tiles.append(a_raw)

        def load_b(jc):
            b_raw = b_in.tile([P, PACK, JC * ND], BF16)
            nc.sync.dma_start(out=b_raw[:], in_=b_rows[:, :, jc * JC * ND : (jc + 1) * JC * ND])
            b_raw_tiles.append(b_raw)

        def transpose_a(it):
            a_raw = a_raw_tiles[it]
            maskT_ps = psum.tile([P, PACK, P], BF16, tag="bank")
            for t in range(PACK):
                nc.tensor.transpose(maskT_ps[:, t, :], mik[:, it, t * P : (t + 1) * P], ident_bf16[:])
            nc.scalar.copy(out=mikT[:, it, :, :], in_=maskT_ps[:].rearrange("p t i -> p i t"))

            a_words = a_raw[:].bitcast(F32).rearrange("p (k w) -> p k w", w=HALF)
            a_grouped = a_work.tile([P, ND, P, PACK], BF16, align_bytes=64)
            a_grouped_tiles.append(a_grouped)
            pair_mask = mikT[:, it, :, :].unsqueeze(1).to_broadcast([P, 2, P, PACK])
            for w in range(HALF):
                aT_ps = psum.tile([P, PACK * P], F32, tag="bank")
                for t in range(PACK):
                    nc.tensor.transpose(
                        aT_ps[:, t * P : (t + 1) * P], a_words[:, t * P : (t + 1) * P, w], ident_f32[:]
                    )
                pair = a_grouped[:, 2 * w : 2 * w + 2, :, :]
                pair_T = aT_ps[:].bitcast(BF16).rearrange("p (t i e) -> p e i t", t=PACK, e=2)
                if w == 0:
                    nc.scalar.copy(out=pair, in_=pair_T)
                else:
                    nc.vector.tensor_tensor(out=pair, in0=pair_T, in1=pair_mask, op=ALU.mult)

        def mask_first_pair_of_a(it):
            pair = a_grouped_tiles[it][:, 0:2, :, :]
            pair_mask = mikT[:, it, :, :].unsqueeze(1).to_broadcast([P, 2, P, PACK])
            nc.vector.tensor_tensor(out=pair, in0=pair, in1=pair_mask, op=ALU.mult)

        def quantise_a(it):
            nc.vector.quantize_mx(
                out=a_codes[:, it, :].bitcast(FP8X4),
                scales=a_scales[:, it, :],
                in_=a_grouped_tiles[it][:].rearrange("p d i t -> p (d i t)"),
            )

        def prepare_a_pair(ip):
            tiles = range(ip * PAIR, (ip + 1) * PAIR)
            for it in tiles:
                transpose_a(it)
                if it + LOADS_AHEAD < I_TILES:
                    load_a(it + LOADS_AHEAD)
            for it in tiles:
                mask_first_pair_of_a(it)
            for it in tiles:
                quantise_a(it)

        def regroup_b(jc):
            b_raw = b_raw_tiles[jc]
            b_grouped = b_work.tile([P, ND, JC, PACK], BF16, align_bytes=64)
            src = b_raw[:].rearrange("p t (j d) -> p j t d", d=ND)
            dst = b_grouped[:].rearrange("p d j t -> p j t d")
            for h in range(2):
                half = slice(h * HALF, (h + 1) * HALF)
                nc.scalar.copy(out=dst[:, :, :, half], in_=src[:, :, :, half])
            b_grouped_tiles.append(b_grouped)
            if jc + LOADS_AHEAD < J_CHUNKS:
                load_b(jc + LOADS_AHEAD)

        def quantise_b(jc):
            b_grouped = b_grouped_tiles[jc]
            b_flat = b_grouped[:].rearrange("p d j t -> p d (j t)")
            nc.vector.tensor_tensor(
                out=b_flat,
                in0=b_flat,
                in1=mkj_grouped[:, jc * JC : (jc + 1) * JC, :]
                .rearrange("p j t -> p (j t)")
                .unsqueeze(1)
                .to_broadcast([P, ND, JC * PACK]),
                op=ALU.mult,
            )
            b_codes = b_mx.tile([P, ND, JC], U32, align_bytes=64)
            b_scales = b_mx.tile([P, ND, JC], U8, align_bytes=64)
            nc.vector.quantize_mx(
                out=b_codes[:].rearrange("p d j -> p (d j)").bitcast(FP8X4),
                scales=b_scales[:].rearrange("p d j -> p (d j)"),
                in_=b_grouped[:].rearrange("p d j t -> p (d j t)"),
            )
            quantised_b.append((b_codes, b_scales))

        blocks = [(ip, jc) for jc in range(J_CHUNKS) for ip in range(I_PAIRS)]
        tiles_of = [dict() for block in blocks]

        def product(where, block, n, d, first, last):
            ip, jc = block
            it = ip * PAIR + n
            b_codes, b_scales = quantised_b[jc]
            nc.tensor.matmul_mx(
                out=where[:, n * JC : (n + 1) * JC],
                lhsT=a_codes[:, it, d * P : (d + 1) * P].bitcast(FP8X4),
                lhsT_scale=a_scales[:, it, d * P : (d + 1) * P],
                rhs=b_codes[:, d, :].bitcast(FP8X4),
                rhs_scale=b_scales[:, d, :],
                start=first,
                stop=last,
            )

        def products_of_two_channels(block, q):
            x_ps = psum.tile([P, 2, BLOCK], F32, tag="bank")
            for e in range(2):
                for n in range(PAIR):
                    product(x_ps[:, e, :], block, n, 2 * q + e, True, True)
            return x_ps

        def sums_and_squares(m):
            sum_ps = psum.tile([P, BLOCK], F32, tag="bank")
            for n in range(PAIR):
                for d in range(ND):
                    product(sum_ps, blocks[m], n, d, d == 0, d == ND - 1)
            mean_sq = ln.tile([P, BLOCK], F32)
            nc.scalar.activation(out=mean_sq[:], in_=sum_ps[:], func=ACT.Square, scale=1.0 / ND)
            neg_mean = ln.tile([P, BLOCK], F32)
            nc.scalar.activation(out=neg_mean[:], in_=sum_ps[:], func=ACT.Copy, scale=-1.0 / ND)
            squares = planes.tile([P, ND, BLOCK], F32)
            for q in range(HALF):
                x_ps = products_of_two_channels(blocks[m], q)
                nc.scalar.activation(out=squares[:, 2 * q : 2 * q + 2, :], in_=x_ps[:], func=ACT.Square)
            tiles_of[m].update(mean_sq=mean_sq, neg_mean=neg_mean, squares=squares)

        def add_squares(m):
            squares = tiles_of[m]["squares"]
            sum_sq_T_ps = psum.tile([P, BLOCK], F32, tag="bank")
            for n in range(PAIR):
                cols = slice(n * JC, (n + 1) * JC)
                for d in range(ND):
                    nc.tensor.matmul(
                        out=sum_sq_T_ps[:, cols],
                        lhsT=squares[:, d, cols],
                        rhs=ident_f32[:],
                        is_transpose=True,
                        start=(d == 0),
                        stop=(d == ND - 1),
                    )
            tiles_of[m].update(sum_sq_T_ps=sum_sq_T_ps)

        def copy_sum_of_squares(m):
            sum_sq_T = ln.tile([P, BLOCK], F32)
            nc.scalar.copy(out=sum_sq_T[:], in_=tiles_of[m]["sum_sq_T_ps"][:])
            tiles_of[m].update(sum_sq_T=sum_sq_T)

        def transpose_sum_of_squares_back(m):
            sum_sq_T = tiles_of[m]["sum_sq_T"]
            sum_sq_ps = psum.tile([P, BLOCK], F32, tag="bank")
            for n in range(PAIR):
                cols = slice(n * JC, (n + 1) * JC)
                nc.tensor.transpose(sum_sq_ps[:, cols], sum_sq_T[:, cols], ident_f32[:])
            tiles_of[m].update(sum_sq_ps=sum_sq_ps)

        def variance(m):
            var = ln.tile([P, BLOCK], F32)
            nc.vector.scalar_tensor_tensor(
                out=var[:],
                in0=tiles_of[m]["sum_sq_ps"][:],
                scalar=1.0 / ND,
                in1=tiles_of[m]["mean_sq"][:],
                op0=ALU.mult,
                op1=ALU.subtract,
            )
            tiles_of[m].update(var=var)

        def reciprocal_std(m):
            rstd = ln.tile([P, BLOCK], F32)
            nc.scalar.activation(
                out=rstd[:], in_=tiles_of[m]["var"][:], func=ACT.Abs_reciprocal_sqrt, bias=eps_col[:, 0:1]
            )
            tiles_of[m].update(rstd=rstd)

        def minus_mean_times_rstd(m):
            neg_mean_rstd = ln.tile([P, BLOCK], F32)
            nc.vector.tensor_tensor(
                out=neg_mean_rstd[:], in0=tiles_of[m]["neg_mean"][:], in1=tiles_of[m]["rstd"][:], op=ALU.mult
            )
            tiles_of[m].update(neg_mean_rstd=neg_mean_rstd)

        def shifts(m):
            shift = planes.tile([P, ND, BLOCK], F32)
            for d in range(HALF):
                nc.scalar.activation(
                    out=shift[:, d, :],
                    in_=tiles_of[m]["neg_mean_rstd"][:],
                    func=ACT.Identity,
                    scale=w_col[:, d : d + 1],
                    bias=bias_col[:, d : d + 1],
                )
            for d in range(HALF, ND):
                nc.vector.tensor_scalar(
                    out=shift[:, d, :],
                    in0=tiles_of[m]["neg_mean_rstd"][:],
                    scalar1=w_col[:, d : d + 1],
                    scalar2=bias_col[:, d : d + 1],
                    op0=ALU.mult,
                    op1=ALU.add,
                )
            tiles_of[m].update(shift=shift)

        def scale_products(m):
            scaled = planes.tile([P, ND, BLOCK], F32, bufs=1)
            for q in range(HALF):
                x_ps = products_of_two_channels(blocks[m], q)
                for e in range(2):
                    d = 2 * q + e
                    nc.vector.scalar_tensor_tensor(
                        out=scaled[:, d, :],
                        in0=x_ps[:, e, :],
                        scalar=w_col[:, d : d + 1],
                        in1=tiles_of[m]["rstd"][:],
                        op0=ALU.mult,
                        op1=ALU.mult,
                    )
            tiles_of[m].update(scaled=scaled)

        def add_shifts_and_store(m):
            ip, jc = blocks[m]
            for n in range(PAIR):
                cols = slice(n * JC, (n + 1) * JC)
                result = results.tile([P, JC, ND], F32)
                nc.vector.tensor_tensor(
                    out=result[:].rearrange("p (c e) d -> p c d e", e=2),
                    in0=tiles_of[m]["scaled"][:, :, cols].rearrange("p d (c e) -> p c d e", e=2),
                    in1=tiles_of[m]["shift"][:, :, cols].rearrange("p d (c e) -> p c d e", e=2),
                    op=ALU.add,
                )
                nc.sync.dma_start(
                    out=out_rows[ip * PAIR + n, :, jc * JC * ND : (jc + 1) * JC * ND],
                    in_=result[:].rearrange("p j d -> p (j d)"),
                )

        load_a(0)
        load_a(1)
        nc.sync.dma_start(out=mkj[:], in_=mkj_rows)
        load_b(0)
        load_a(2)
        load_b(1)
        load_b(2)

        prepare_a_pair(0)
        nc.scalar.copy(out=mkj_grouped[:], in_=mkj[:].rearrange("p t j -> p j t"))
        regroup_b(0)
        quantise_b(0)
        prepare_a_pair(1)
        for jc in range(1, J_CHUNKS):
            regroup_b(jc)
            quantise_b(jc)
        nc.vector.tensor_copy(out=w_col[:], in_=w_bf16[:])
        nc.vector.tensor_copy(out=bias_col[:], in_=bias_bf16[:])

        def stage(work, m):
            if 0 <= m < len(blocks):
                work(m)

        for m in range(-4, len(blocks)):
            stage(scale_products, m)
            stage(add_squares, m + 2)
            stage(copy_sum_of_squares, m + 2)
            stage(minus_mean_times_rstd, m + 1)
            stage(add_shifts_and_store, m)
            stage(sums_and_squares, m + 4)
            stage(transpose_sum_of_squares_back, m + 2)
            stage(variance, m + 2)
            stage(reciprocal_std, m + 2)
            stage(shifts, m + 1)
